import numpy as np
import ml_dtypes


def mxq(x, axis, fmt="e4m3"):
    dtype, down = {"e4m3": (ml_dtypes.float8_e4m3fn, 7), "e5m2": (ml_dtypes.float8_e5m2, 14)}[fmt]
    v = np.moveaxis(np.asarray(x, np.float32).astype(ml_dtypes.bfloat16).astype(np.float64), axis, -1)
    blocks = v.reshape(v.shape[:-1] + (-1, 32))
    amax = np.abs(blocks).max(-1, keepdims=True)
    byte = np.maximum(np.where(amax > 0, np.frexp(amax)[1] - 1 + 127, 0) - down, 1)
    scale = np.exp2(byte - 127.0)
    codes = (blocks / scale).astype(np.float32).astype(dtype).astype(np.float64)
    return np.moveaxis((codes * scale).reshape(v.shape), -1, axis)


WIDE = False


def mx_kscale(k):
    if not WIDE:
        return np.ones(k)
    levels = np.array([10, -10, 5, -5, 0])
    a = np.random.permutation(np.resize(levels, k // 512 * 4)).reshape(k // 512, 4)
    idx = np.arange(k)
    return np.exp2(a[idx // 512, idx % 128 // 32])


BF16 = ml_dtypes.bfloat16


def bf(x):
    return np.asarray(x, np.float32).astype(BF16)


def f64(x):
    return np.asarray(x).astype(np.float64)


NP, NH, NF, NU, B, C, H, W, IN_DIM = 7, 3, 2, 4, 8, 512, 8, 16, 256
S = H * W
EPS = 1e-5


def make_bn():
    return bf(np.stack([1.0 + 0.1 * np.random.standard_normal(C), 0.1 * np.random.standard_normal(C),
                        0.1 * np.random.standard_normal(C), np.random.uniform(0.5, 1.5, C)]))


def make_w(col):
    return bf(np.random.standard_normal((C, col.size)) / np.sqrt(col.size) / col)


def make_nodes(n, s):
    return bf(np.random.standard_normal((n, B, C, H, W)) * s[:, None, None])


def setup_inputs():
    s = mx_kscale(C)
    return {'p_nodes': make_nodes(NP, s), 'h_nodes': make_nodes(NH, s),
            'W_decomp_half': make_w(np.concatenate([s, s])), 'bn_decomp_half': make_bn(),
            'W_bg_p': make_w(np.concatenate([s, s])), 'bn_bg_p': make_bn()}


def conv(wq, xs):
    y, c0 = 0.0, 0
    for x in xs:
        c1 = c0 + x.shape[1]
        y = y + (wq[:, c0:c1] @ x)
        c0 = c1
    return y


def bn_relu(y, bn):
    gamma, beta, mean, var = f64(bn)
    scale = gamma / np.sqrt(var + EPS)
    shift = beta - mean * scale
    return np.maximum(y * scale[:, None] + shift[:, None], 0.0)


def reference(p_nodes, h_nodes, W_decomp_half, bn_decomp_half, W_bg_p, bn_bg_p):
    pq = mxq(f64(p_nodes).reshape(NP, B, C, S), 2, 'e4m3')
    hq = mxq(f64(h_nodes).reshape(NH, B, C, S), 2, 'e4m3')
    wd = mxq(f64(W_decomp_half), 1, 'e4m3')
    wb = mxq(f64(W_bg_p), 1, 'e4m3')
    p0 = bn_relu(conv(wb, [hq[0], pq[0]]), bn_bg_p)
    p_up = [bn_relu(conv(wd, [hq[1], pq[n]]), bn_decomp_half) for n in range(1, 1 + NU)]
    p_lo = [bn_relu(conv(wd, [hq[2], pq[n]]), bn_decomp_half) for n in range(1 + NU, NP)]
    return np.stack([p0] + p_up + p_lo).reshape(NP, B, C, H, W)

@@ -1,0 +1,147 @@
+from contextlib import ExitStack
+
+import concourse.mybir as mybir
+from concourse.masks import make_identity
+
+BF16 = mybir.dt.bfloat16
+F32 = mybir.dt.float32
+U32 = mybir.dt.uint32
+U8 = mybir.dt.uint8
+FP8X4 = mybir.dt.float8_e4m3fn_x4
+ACT = mybir.ActivationFunctionType
+
+P = 128
+PACK = 4
+N_PART, N_HALF_BODY, IMAGES, CHANNELS, PIXELS = 7, 3, 8, 512, 128
+EPS = 1e-5
+assert CHANNELS == P * PACK
+
+SOURCES = 2
+OUT_TILES = CHANNELS // P
+GROUP = 4
+GROUPS = IMAGES // GROUP
+COLS = GROUP * PIXELS
+
+FLOPS = 2 * N_PART * IMAGES * PIXELS * CHANNELS * SOURCES * CHANNELS
+
+
+def batch_norm_affine(nc, small, bn, label):
+    rows_bf16 = small.tile([P, 4, OUT_TILES], BF16, name="rows_bf16_" + label)
+    nc.scalar.dma_start(out=rows_bf16[:], in_=bn.rearrange("r (m j) -> m r j", j=OUT_TILES))
+    rows = small.tile([P, 4, OUT_TILES], F32, name="rows_" + label)
+    nc.vector.tensor_copy(out=rows[:], in_=rows_bf16[:])
+    gamma, beta, mean, var = rows[:, 0, :], rows[:, 1, :], rows[:, 2, :], rows[:, 3, :]
+    std = small.tile([P, OUT_TILES], F32, name="std_" + label)
+    scale = small.tile([P, OUT_TILES], F32, name="scale_" + label)
+    shift = small.tile([P, OUT_TILES], F32, name="shift_" + label)
+    nc.vector.tensor_scalar_add(out=std[:], in0=var, scalar1=EPS)
+    nc.scalar.sqrt(out=std[:], in_=std[:])
+    nc.vector.reciprocal(out=scale[:], in_=std[:])
+    nc.vector.tensor_mul(out=scale[:], in0=scale[:], in1=gamma)
+    nc.vector.tensor_mul(out=shift[:], in0=mean, in1=scale[:])
+    nc.vector.tensor_sub(out=shift[:], in0=beta, in1=shift[:])
+    return scale, shift
+
+
+def quantise_weight(nc, keep, stage, psum_t, identity, weight, label):
+    raw = keep.tile([P, OUT_TILES * SOURCES * CHANNELS], BF16, name="w_raw_" + label)
+    nc.sync.dma_start(out=raw[:], in_=weight.rearrange("(m j) c -> m (j c)", j=OUT_TILES))
+    words = raw[:].bitcast(F32).rearrange("m (j g p u) -> m j g u p", j=OUT_TILES, g=SOURCES, u=2)
+    codes = keep.tile([P, SOURCES, OUT_TILES * P], U32, name="w_codes_" + label, align_bytes=64)
+    scales = keep.tile([P, SOURCES, OUT_TILES * P], U8, name="w_scales_" + label, align_bytes=64)
+    for g in range(SOURCES):
+        grouped = stage.tile([P, OUT_TILES * P * PACK], BF16, name="w_grouped", align_bytes=64)
+        grouped_words = grouped[:].bitcast(F32).rearrange("p (j m u) -> p j m u", j=OUT_TILES, u=2)
+        for pair in range(OUT_TILES // 2):
+            bank = psum_t.tile([P, 2, 2, P], F32, name="w_bank")
+            for i in range(2):
+                for u in range(2):
+                    nc.tensor.transpose(bank[:, i, u, :], words[:, 2 * pair + i, g, u, :], identity[:])
+            copy = nc.vector.tensor_copy if pair == 0 else nc.scalar.copy
+            copy(
+                out=grouped_words[:, 2 * pair : 2 * pair + 2, :, :],
+                in_=bank[:].rearrange("p i u m -> p i m u"),
+            )
+        nc.vector.quantize_mx(out=codes[:, g, :].bitcast(FP8X4), scales=scales[:, g, :], in_=grouped[:])
+    return codes, scales
+
+
+def quantise_maps(nc, raw_pool, stage, code_pool, maps, label):
+    raw = raw_pool.tile([P, GROUP, PACK, PIXELS], BF16, name="raw")
+    nc.sync.dma_start(out=raw[:], in_=maps.rearrange("b (p t) h w -> p b t (h w)", t=PACK))
+    grouped = stage.tile([P, GROUP, PIXELS, PACK], BF16, name="grouped", align_bytes=64)
+    nc.vector.tensor_copy(out=grouped[:], in_=raw[:].rearrange("p b t s -> p b s t"))
+    codes = code_pool.tile([P, COLS], U32, name="codes_" + label, align_bytes=64)
+    scales = code_pool.tile([P, COLS], U8, name="scales_" + label, align_bytes=64)
+    nc.vector.quantize_mx(
+        out=codes[:].bitcast(FP8X4),
+        scales=scales[:],
+        in_=grouped[:].rearrange("p b s t -> p (b s t)"),
+    )
+    return codes, scales
+
+
+def tile_gnn_pb_kernel(
+    tc, p_nodes, h_nodes, W_decomp_half, bn_decomp_half, W_bg_p, bn_bg_p, out
+):
+    nc = tc.nc
+    with ExitStack() as ctx:
+        small = ctx.enter_context(tc.tile_pool(name="small", bufs=1))
+        keep = ctx.enter_context(tc.tile_pool(name="keep", bufs=1))
+        raw_pool = ctx.enter_context(tc.tile_pool(name="raw_pool", bufs=12))
+        stage = ctx.enter_context(tc.tile_pool(name="stage", bufs=3))
+        parent_codes = ctx.enter_context(tc.tile_pool(name="parent_codes", bufs=2 * GROUPS))
+        part_codes = ctx.enter_context(tc.tile_pool(name="part_codes", bufs=4))
+        results = ctx.enter_context(tc.tile_pool(name="results", bufs=10))
+        psum_t = ctx.enter_context(tc.psum_pool(name="psum_t", bufs=2))
+        psum_acc = ctx.enter_context(tc.psum_pool(name="psum_acc", bufs=6))
+
+        identity = small.tile([P, P], F32, name="identity")
+        make_identity(nc, identity[:])
+        affine_bg = batch_norm_affine(nc, small, bn_bg_p, "bg")
+        affine_decomp = batch_norm_affine(nc, small, bn_decomp_half, "decomp")
+
+        def update_parts(parent, parts, weight, affine):
+            w_codes, w_scales = weight
+            scale, shift = affine
+            parent_q = [
+                quantise_maps(
+                    nc, raw_pool, stage, parent_codes,
+                    h_nodes[parent, GROUP * i : GROUP * (i + 1)], "parent",
+                )
+                for i in range(GROUPS)
+            ]
+            for n in parts:
+                for i in range(GROUPS):
+                    images = slice(GROUP * i, GROUP * (i + 1))
+                    part_q = quantise_maps(nc, raw_pool, stage, part_codes, p_nodes[n, images], "part")
+                    result = results.tile([P, GROUP, OUT_TILES, PIXELS], F32, name="result")
+                    for j in range(OUT_TILES):
+                        acc = psum_acc.tile([P, COLS], F32, name="acc")
+                        for g, (codes, scales) in enumerate((parent_q[i], part_q)):
+                            nc.tensor.matmul_mx(
+                                out=acc[:],
+                                lhsT=w_codes[:, g, P * j : P * (j + 1)].bitcast(FP8X4),
+                                lhsT_scale=w_scales[:, g, P * j : P * (j + 1)],
+                                rhs=codes[:].bitcast(FP8X4),
+                                rhs_scale=scales[:],
+                                start=(g == 0),
+                                stop=(g == SOURCES - 1),
+                            )
+                        nc.scalar.activation(
+                            out=result[:, :, j, :],
+                            in_=acc[:].rearrange("m (b s) -> m b s", s=PIXELS),
+                            func=ACT.Relu,
+                            bias=shift[:, j : j + 1],
+                            scale=scale[:, j : j + 1],
+                        )
+                    nc.scalar.dma_start(
+                        out=out[n, images].rearrange("b (m j) h w -> m b (j h w)", j=OUT_TILES),
+                        in_=result[:].rearrange("m b j s -> m b (j s)"),
+                    )
+
+        weight_bg = quantise_weight(nc, keep, stage, psum_t, identity, W_bg_p, "bg")
+        update_parts(0, (0,), weight_bg, affine_bg)
+        weight_decomp = quantise_weight(nc, keep, stage, psum_t, identity, W_decomp_half, "decomp")
+        update_parts(1, (1, 2, 3, 4), weight_decomp, affine_decomp)
+        update_parts(2, (5, 6), weight_decomp, affine_decomp)

@@ -14,6 +14,7 @@ P = 128
 PACK = 4
 N_PART, N_HALF_BODY, IMAGES, CHANNELS, PIXELS = 7, 3, 8, 512, 128
 EPS = 1e-5
+BN_ROWS = 4
 assert CHANNELS == P * PACK
 
 SOURCES = 2
@@ -25,15 +26,24 @@ COLS = GROUP * PIXELS
 FLOPS = 2 * N_PART * IMAGES * PIXELS * CHANNELS * SOURCES * CHANNELS
 
 
-def batch_norm_affine(nc, small, bn, label):
-    rows_bf16 = small.tile([P, 4, OUT_TILES], BF16, name="rows_bf16_" + label)
-    nc.scalar.dma_start(out=rows_bf16[:], in_=bn.rearrange("r (m j) -> m r j", j=OUT_TILES))
-    rows = small.tile([P, 4, OUT_TILES], F32, name="rows_" + label)
-    nc.vector.tensor_copy(out=rows[:], in_=rows_bf16[:])
-    gamma, beta, mean, var = rows[:, 0, :], rows[:, 1, :], rows[:, 2, :], rows[:, 3, :]
-    std = small.tile([P, OUT_TILES], F32, name="std_" + label)
-    scale = small.tile([P, OUT_TILES], F32, name="scale_" + label)
-    shift = small.tile([P, OUT_TILES], F32, name="shift_" + label)
+def batch_norm_affine(nc, small, psum_t, identity, batch_norms):
+    count = len(batch_norms)
+    table = small.tile([P, CHANNELS], BF16, name="bn_table")
+    nc.vector.memset(table[:], 0.0)
+    for i, bn in enumerate(batch_norms):
+        nc.scalar.dma_start(out=table[BN_ROWS * i : BN_ROWS * (i + 1), :], in_=bn)
+    words = table[:].bitcast(F32).rearrange("r (m u) -> r u m", u=2)
+    turned = psum_t.tile([P, 2 * P], F32, name="bn_turned", tag="turned")
+    for u in range(2):
+        nc.tensor.transpose(turned[:, P * u : P * (u + 1)], words[:, u, :], identity[:])
+    rows = small.tile([P, BN_ROWS * count, 2, 2], F32, name="bn_rows")
+    pairs = turned[:].bitcast(BF16).rearrange("m (u r e) -> m r u e", u=2, e=2)
+    nc.vector.tensor_copy(out=rows[:], in_=pairs[:, 0 : BN_ROWS * count, :, :])
+    by_norm = rows[:].rearrange("m (i r) u e -> m r i (u e)", r=BN_ROWS)
+    gamma, beta, mean, var = by_norm[:, 0], by_norm[:, 1], by_norm[:, 2], by_norm[:, 3]
+    std = small.tile([P, count, OUT_TILES], F32, name="bn_std")
+    scale = small.tile([P, count, OUT_TILES], F32, name="bn_scale")
+    shift = small.tile([P, count, OUT_TILES], F32, name="bn_shift")
     nc.vector.tensor_scalar_add(out=std[:], in0=var, scalar1=EPS)
     nc.scalar.sqrt(out=std[:], in_=std[:])
     nc.vector.reciprocal(out=scale[:], in_=std[:])
@@ -53,7 +63,7 @@ def quantise_weight(nc, keep, stage, psum_t, identity, weight, label):
         grouped = stage.tile([P, OUT_TILES * P * PACK], BF16, name="w_grouped", align_bytes=64)
         grouped_words = grouped[:].bitcast(F32).rearrange("p (j m u) -> p j m u", j=OUT_TILES, u=2)
         for pair in range(OUT_TILES // 2):
-            bank = psum_t.tile([P, 2, 2, P], F32, name="w_bank")
+            bank = psum_t.tile([P, 2, 2, P], F32, name="w_bank", tag="turned")
             for i in range(2):
                 for u in range(2):
                     nc.tensor.transpose(bank[:, i, u, :], words[:, 2 * pair + i, g, u, :], identity[:])
@@ -98,8 +108,9 @@ def tile_gnn_pb_kernel(
 
         identity = small.tile([P, P], F32, name="identity")
         make_identity(nc, identity[:])
-        affine_bg = batch_norm_affine(nc, small, bn_bg_p, "bg")
-        affine_decomp = batch_norm_affine(nc, small, bn_decomp_half, "decomp")
+        bn_scale, bn_shift = batch_norm_affine(nc, small, psum_t, identity, (bn_bg_p, bn_decomp_half))
+        affine_bg = (bn_scale[:, 0, :], bn_shift[:, 0, :])
+        affine_decomp = (bn_scale[:, 1, :], bn_shift[:, 1, :])
 
         def update_parts(parent, parts, weight, affine):
             w_codes, w_scales = weight

@@ -76,11 +76,15 @@ def quantise_weight(nc, keep, stage, psum_t, identity, weight, label):
     return codes, scales
 
 
-def quantise_maps(nc, raw_pool, stage, code_pool, maps, label):
+def group_maps(nc, raw_pool, stage, maps):
     raw = raw_pool.tile([P, GROUP, PACK, PIXELS], BF16, name="raw")
     nc.sync.dma_start(out=raw[:], in_=maps.rearrange("b (p t) h w -> p b t (h w)", t=PACK))
     grouped = stage.tile([P, GROUP, PIXELS, PACK], BF16, name="grouped", align_bytes=64)
     nc.vector.tensor_copy(out=grouped[:], in_=raw[:].rearrange("p b t s -> p b s t"))
+    return grouped
+
+
+def quantise_maps(nc, code_pool, grouped, label):
     codes = code_pool.tile([P, COLS], U32, name="codes_" + label, align_bytes=64)
     scales = code_pool.tile([P, COLS], U8, name="scales_" + label, align_bytes=64)
     nc.vector.quantize_mx(
@@ -112,47 +116,58 @@ def tile_gnn_pb_kernel(
         affine_bg = (bn_scale[:, 0, :], bn_shift[:, 0, :])
         affine_decomp = (bn_scale[:, 1, :], bn_shift[:, 1, :])
 
-        def update_parts(parent, parts, weight, affine):
+        steps = []
+        for parent, parts in ((0, (0,)), (1, (1, 2, 3, 4)), (2, (5, 6))):
+            steps.extend([(parent, None, i) for i in range(GROUPS)])
+            steps.extend([(parent, n, i) for n in parts for i in range(GROUPS)])
+
+        def group_step(step):
+            parent, n, i = step
+            node = h_nodes[parent] if n is None else p_nodes[n]
+            return group_maps(nc, raw_pool, stage, node[GROUP * i : GROUP * (i + 1)])
+
+        def update_part(n, i, parent_q, part_q, weight, affine):
             w_codes, w_scales = weight
             scale, shift = affine
-            parent_q = [
-                quantise_maps(
-                    nc, raw_pool, stage, parent_codes,
-                    h_nodes[parent, GROUP * i : GROUP * (i + 1)], "parent",
-                )
-                for i in range(GROUPS)
-            ]
-            for n in parts:
-                for i in range(GROUPS):
-                    images = slice(GROUP * i, GROUP * (i + 1))
-                    part_q = quantise_maps(nc, raw_pool, stage, part_codes, p_nodes[n, images], "part")
-                    result = results.tile([P, GROUP, OUT_TILES, PIXELS], F32, name="result")
-                    for j in range(OUT_TILES):
-                        acc = psum_acc.tile([P, COLS], F32, name="acc")
-                        for g, (codes, scales) in enumerate((parent_q[i], part_q)):
-                            nc.tensor.matmul_mx(
-                                out=acc[:],
-                                lhsT=w_codes[:, g, P * j : P * (j + 1)].bitcast(FP8X4),
-                                lhsT_scale=w_scales[:, g, P * j : P * (j + 1)],
-                                rhs=codes[:].bitcast(FP8X4),
-                                rhs_scale=scales[:],
-                                start=(g == 0),
-                                stop=(g == SOURCES - 1),
-                            )
-                        nc.scalar.activation(
-                            out=result[:, :, j, :],
-                            in_=acc[:].rearrange("m (b s) -> m b s", s=PIXELS),
-                            func=ACT.Relu,
-                            bias=shift[:, j : j + 1],
-                            scale=scale[:, j : j + 1],
-                        )
-                    nc.scalar.dma_start(
-                        out=out[n, images].rearrange("b (m j) h w -> m b (j h w)", j=OUT_TILES),
-                        in_=result[:].rearrange("m b j s -> m b (j s)"),
+            images = slice(GROUP * i, GROUP * (i + 1))
+            result = results.tile([P, GROUP, OUT_TILES, PIXELS], F32, name="result")
+            for j in range(OUT_TILES):
+                acc = psum_acc.tile([P, COLS], F32, name="acc")
+                for g, (codes, scales) in enumerate((parent_q, part_q)):
+                    nc.tensor.matmul_mx(
+                        out=acc[:],
+                        lhsT=w_codes[:, g, P * j : P * (j + 1)].bitcast(FP8X4),
+                        lhsT_scale=w_scales[:, g, P * j : P * (j + 1)],
+                        rhs=codes[:].bitcast(FP8X4),
+                        rhs_scale=scales[:],
+                        start=(g == 0),
+                        stop=(g == SOURCES - 1),
                     )
+                nc.scalar.activation(
+                    out=result[:, :, j, :],
+                    in_=acc[:].rearrange("m (b s) -> m b s", s=PIXELS),
+                    func=ACT.Relu,
+                    bias=shift[:, j : j + 1],
+                    scale=scale[:, j : j + 1],
+                )
+            nc.scalar.dma_start(
+                out=out[n, images].rearrange("b (m j) h w -> m b (j h w)", j=OUT_TILES),
+                in_=result[:].rearrange("m b j s -> m b (j s)"),
+            )
 
-        weight_bg = quantise_weight(nc, keep, stage, psum_t, identity, W_bg_p, "bg")
-        update_parts(0, (0,), weight_bg, affine_bg)
-        weight_decomp = quantise_weight(nc, keep, stage, psum_t, identity, W_decomp_half, "decomp")
-        update_parts(1, (1, 2, 3, 4), weight_decomp, affine_decomp)
-        update_parts(2, (5, 6), weight_decomp, affine_decomp)
+        weights = {0: quantise_weight(nc, keep, stage, psum_t, identity, W_bg_p, "bg")}
+        affines = {0: affine_bg, 1: affine_decomp, 2: affine_decomp}
+        parent_q = {}
+        grouped_next = group_step(steps[0])
+        for k, (parent, n, i) in enumerate(steps):
+            grouped = grouped_next
+            if k + 1 < len(steps):
+                grouped_next = group_step(steps[k + 1])
+            if n is None:
+                parent_q[i] = quantise_maps(nc, parent_codes, grouped, "parent")
+                continue
+            part_q = quantise_maps(nc, part_codes, grouped, "part")
+            update_part(n, i, parent_q[i], part_q, weights[parent], affines[parent])
+            if n == 0 and i == GROUPS - 1:
+                weights[1] = quantise_weight(nc, keep, stage, psum_t, identity, W_decomp_half, "decomp")
+                weights[2] = weights[1]

@@ -22,6 +22,7 @@ OUT_TILES = CHANNELS // P
 GROUP = 4
 GROUPS = IMAGES // GROUP
 COLS = GROUP * PIXELS
+DMA_ALIGN = 256
 
 FLOPS = 2 * N_PART * IMAGES * PIXELS * CHANNELS * SOURCES * CHANNELS
 
@@ -54,7 +55,9 @@ def batch_norm_affine(nc, small, psum_t, identity, batch_norms):
 
 
 def quantise_weight(nc, keep, stage, psum_t, identity, weight, label):
-    raw = keep.tile([P, OUT_TILES * SOURCES * CHANNELS], BF16, name="w_raw_" + label)
+    raw = keep.tile(
+        [P, OUT_TILES * SOURCES * CHANNELS], BF16, name="w_raw_" + label, align_bytes=DMA_ALIGN
+    )
     nc.sync.dma_start(out=raw[:], in_=weight.rearrange("(m j) c -> m (j c)", j=OUT_TILES))
     words = raw[:].bitcast(F32).rearrange("m (j g p u) -> m j g u p", j=OUT_TILES, g=SOURCES, u=2)
     codes = keep.tile([P, SOURCES, OUT_TILES * P], U32, name="w_codes_" + label, align_bytes=64)
@@ -77,7 +80,7 @@ def quantise_weight(nc, keep, stage, psum_t, identity, weight, label):
 
 
 def group_maps(nc, raw_pool, stage, maps):
-    raw = raw_pool.tile([P, GROUP, PACK, PIXELS], BF16, name="raw")
+    raw = raw_pool.tile([P, GROUP, PACK, PIXELS], BF16, name="raw", align_bytes=DMA_ALIGN)
     nc.sync.dma_start(out=raw[:], in_=maps.rearrange("b (p t) h w -> p b t (h w)", t=PACK))
     grouped = stage.tile([P, GROUP, PIXELS, PACK], BF16, name="grouped", align_bytes=64)
     nc.vector.tensor_copy(out=grouped[:], in_=raw[:].rearrange("p b t s -> p b s t"))
@@ -130,7 +133,7 @@ def tile_gnn_pb_kernel(
             w_codes, w_scales = weight
             scale, shift = affine
             images = slice(GROUP * i, GROUP * (i + 1))
-            result = results.tile([P, GROUP, OUT_TILES, PIXELS], F32, name="result")
+            result = results.tile([P, GROUP, OUT_TILES, PIXELS], F32, name="result", align_bytes=DMA_ALIGN)
             for j in range(OUT_TILES):
                 acc = psum_acc.tile([P, COLS], F32, name="acc")
                 for g, (codes, scales) in enumerate((parent_q, part_q)):

@@ -30,9 +30,10 @@ FLOPS = 2 * N_PART * IMAGES * PIXELS * CHANNELS * SOURCES * CHANNELS
 def batch_norm_affine(nc, small, psum_t, identity, batch_norms):
     count = len(batch_norms)
     table = small.tile([P, CHANNELS], BF16, name="bn_table")
-    nc.vector.memset(table[:], 0.0)
+    nc.gpsimd.memset(table[:], 0.0)
     for i, bn in enumerate(batch_norms):
-        nc.scalar.dma_start(out=table[BN_ROWS * i : BN_ROWS * (i + 1), :], in_=bn)
+        nc.sync.dma_start(out=table[BN_ROWS * i : BN_ROWS * (i + 1), :], in_=bn)
+    make_identity(nc, identity[:])
     words = table[:].bitcast(F32).rearrange("r (m u) -> r u m", u=2)
     turned = psum_t.tile([P, 2 * P], F32, name="bn_turned", tag="turned")
     for u in range(2):
@@ -113,8 +114,10 @@ def tile_gnn_pb_kernel(
         psum_t = ctx.enter_context(tc.psum_pool(name="psum_t", bufs=2))
         psum_acc = ctx.enter_context(tc.psum_pool(name="psum_acc", bufs=6))
 
+        warm = small.tile([P, 1], F32, name="warm")
+        nc.gpsimd.memset(warm[:], 1.0)
+        nc.scalar.sqrt(out=warm[:], in_=warm[:])
         identity = small.tile([P, P], F32, name="identity")
-        make_identity(nc, identity[:])
         bn_scale, bn_shift = batch_norm_affine(nc, small, psum_t, identity, (bn_bg_p, bn_decomp_half))
         affine_bg = (bn_scale[:, 0, :], bn_shift[:, 0, :])
         affine_decomp = (bn_scale[:, 1, :], bn_shift[:, 1, :])

@@ -156,7 +156,8 @@ def tile_gnn_pb_kernel(
                     bias=shift[:, j : j + 1],
                     scale=scale[:, j : j + 1],
                 )
-            nc.scalar.dma_start(
+            queue = nc.sync if (n >= 2 and i == 1) else nc.scalar
+            queue.dma_start(
                 out=out[n, images].rearrange("b (m j) h w -> m b (j h w)", j=OUT_TILES),
                 in_=result[:].rearrange("m b j s -> m b (j s)"),
             )

@@ -27,13 +27,15 @@ DMA_ALIGN = 256
 FLOPS = 2 * N_PART * IMAGES * PIXELS * CHANNELS * SOURCES * CHANNELS
 
 
-def batch_norm_affine(nc, small, psum_t, identity, batch_norms):
-    count = len(batch_norms)
+def load_batch_norms(nc, small, batch_norms):
     table = small.tile([P, CHANNELS], BF16, name="bn_table")
     nc.gpsimd.memset(table[:], 0.0)
     for i, bn in enumerate(batch_norms):
         nc.sync.dma_start(out=table[BN_ROWS * i : BN_ROWS * (i + 1), :], in_=bn)
-    make_identity(nc, identity[:])
+    return table
+
+
+def batch_norm_affine(nc, small, psum_t, identity, table, count):
     words = table[:].bitcast(F32).rearrange("r (m u) -> r u m", u=2)
     turned = psum_t.tile([P, 2 * P], F32, name="bn_turned", tag="turned")
     for u in range(2):
@@ -55,34 +57,36 @@ def batch_norm_affine(nc, small, psum_t, identity, batch_norms):
     return scale, shift
 
 
-def quantise_weight(nc, keep, stage, psum_t, identity, weight, label):
-    raw = keep.tile(
-        [P, OUT_TILES * SOURCES * CHANNELS], BF16, name="w_raw_" + label, align_bytes=DMA_ALIGN
-    )
-    nc.sync.dma_start(out=raw[:], in_=weight.rearrange("(m j) c -> m (j c)", j=OUT_TILES))
-    words = raw[:].bitcast(F32).rearrange("m (j g p u) -> m j g u p", j=OUT_TILES, g=SOURCES, u=2)
-    codes = keep.tile([P, SOURCES, OUT_TILES * P], U32, name="w_codes_" + label, align_bytes=64)
-    scales = keep.tile([P, SOURCES, OUT_TILES * P], U8, name="w_scales_" + label, align_bytes=64)
+def load_weight_tile(nc, w_raw, weight, label, j):
+    raw = w_raw.tile([P, SOURCES * CHANNELS], BF16, name="w_raw_%s%d" % (label, j), align_bytes=DMA_ALIGN)
+    nc.sync.dma_start(out=raw[:], in_=weight.rearrange("(m j) c -> j m c", j=OUT_TILES)[j])
+    return raw
+
+
+def quantise_weight_tile(nc, keep, stage, psum_t, identity, raw, copy, label):
+    words = raw[:].bitcast(F32).rearrange("m (g p u) -> m g u p", g=SOURCES, u=2)
+    bank = psum_t.tile([P, SOURCES, 2, P], F32, name="w_bank", tag="turned")
     for g in range(SOURCES):
-        grouped = stage.tile([P, OUT_TILES * P * PACK], BF16, name="w_grouped", align_bytes=64)
-        grouped_words = grouped[:].bitcast(F32).rearrange("p (j m u) -> p j m u", j=OUT_TILES, u=2)
-        for pair in range(OUT_TILES // 2):
-            bank = psum_t.tile([P, 2, 2, P], F32, name="w_bank", tag="turned")
-            for i in range(2):
-                for u in range(2):
-                    nc.tensor.transpose(bank[:, i, u, :], words[:, 2 * pair + i, g, u, :], identity[:])
-            copy = nc.vector.tensor_copy if pair == 0 else nc.scalar.copy
-            copy(
-                out=grouped_words[:, 2 * pair : 2 * pair + 2, :, :],
-                in_=bank[:].rearrange("p i u m -> p i m u"),
-            )
-        nc.vector.quantize_mx(out=codes[:, g, :].bitcast(FP8X4), scales=scales[:, g, :], in_=grouped[:])
+        for u in range(2):
+            nc.tensor.transpose(bank[:, g, u, :], words[:, g, u, :], identity[:])
+    grouped = stage.tile([P, SOURCES * P * PACK], BF16, name="w_grouped", align_bytes=64)
+    copy(
+        out=grouped[:].bitcast(F32).rearrange("p (g m u) -> p g m u", g=SOURCES, u=2),
+        in_=bank[:].rearrange("p g u m -> p g m u"),
+    )
+    codes = keep.tile([P, SOURCES * P], U32, name="w_codes_" + label, align_bytes=64)
+    scales = keep.tile([P, SOURCES * P], U8, name="w_scales_" + label, align_bytes=64)
+    nc.vector.quantize_mx(out=codes[:].bitcast(FP8X4), scales=scales[:], in_=grouped[:])
     return codes, scales
 
 
-def group_maps(nc, raw_pool, stage, maps):
+def load_maps(nc, raw_pool, maps):
     raw = raw_pool.tile([P, GROUP, PACK, PIXELS], BF16, name="raw", align_bytes=DMA_ALIGN)
     nc.sync.dma_start(out=raw[:], in_=maps.rearrange("b (p t) h w -> p b t (h w)", t=PACK))
+    return raw
+
+
+def group_maps(nc, stage, raw):
     grouped = stage.tile([P, GROUP, PIXELS, PACK], BF16, name="grouped", align_bytes=64)
     nc.vector.tensor_copy(out=grouped[:], in_=raw[:].rearrange("p b t s -> p b s t"))
     return grouped
@@ -114,36 +118,47 @@ def tile_gnn_pb_kernel(
         psum_t = ctx.enter_context(tc.psum_pool(name="psum_t", bufs=2))
         psum_acc = ctx.enter_context(tc.psum_pool(name="psum_acc", bufs=6))
 
+        steps = [(0, n, i) for i in range(GROUPS) for n in (None, 0)]
+        for parent, parts in ((1, (1, 2, 3, 4)), (2, (5, 6))):
+            steps.extend([(parent, n, i) for n in (None, *parts) for i in range(GROUPS)])
+
+        def load_step(k):
+            parent, n, i = steps[k]
+            node = h_nodes[parent] if n is None else p_nodes[n]
+            return load_maps(nc, raw_pool, node[GROUP * i : GROUP * (i + 1)])
+
+        raw_bg, early = [], []
+        for j in range(OUT_TILES):
+            raw_bg.append(load_weight_tile(nc, keep, W_bg_p, "bg", j))
+            if j == 0:
+                bn_table = load_batch_norms(nc, small, (bn_bg_p, bn_decomp_half))
+            if j % 2 == 1:
+                early.append(load_step(len(early)))
+
         warm = small.tile([P, 1], F32, name="warm")
         nc.gpsimd.memset(warm[:], 1.0)
         nc.scalar.sqrt(out=warm[:], in_=warm[:])
         identity = small.tile([P, P], F32, name="identity")
-        bn_scale, bn_shift = batch_norm_affine(nc, small, psum_t, identity, (bn_bg_p, bn_decomp_half))
+        make_identity(nc, identity[:])
+        bn_scale, bn_shift = batch_norm_affine(nc, small, psum_t, identity, bn_table, 2)
         affine_bg = (bn_scale[:, 0, :], bn_shift[:, 0, :])
         affine_decomp = (bn_scale[:, 1, :], bn_shift[:, 1, :])
 
-        steps = []
-        for parent, parts in ((0, (0,)), (1, (1, 2, 3, 4)), (2, (5, 6))):
-            steps.extend([(parent, None, i) for i in range(GROUPS)])
-            steps.extend([(parent, n, i) for n in parts for i in range(GROUPS)])
-
-        def group_step(step):
-            parent, n, i = step
-            node = h_nodes[parent] if n is None else p_nodes[n]
-            return group_maps(nc, raw_pool, stage, node[GROUP * i : GROUP * (i + 1)])
+        def group_step(k):
+            return group_maps(nc, stage, early[k] if k < len(early) else load_step(k))
 
         def update_part(n, i, parent_q, part_q, weight, affine):
-            w_codes, w_scales = weight
             scale, shift = affine
             images = slice(GROUP * i, GROUP * (i + 1))
             result = results.tile([P, GROUP, OUT_TILES, PIXELS], F32, name="result", align_bytes=DMA_ALIGN)
             for j in range(OUT_TILES):
+                w_codes, w_scales = weight[j]
                 acc = psum_acc.tile([P, COLS], F32, name="acc")
                 for g, (codes, scales) in enumerate((parent_q, part_q)):
                     nc.tensor.matmul_mx(
                         out=acc[:],
-                        lhsT=w_codes[:, g, P * j : P * (j + 1)].bitcast(FP8X4),
-                        lhsT_scale=w_scales[:, g, P * j : P * (j + 1)],
+                        lhsT=w_codes[:, P * g : P * (g + 1)].bitcast(FP8X4),
+                        lhsT_scale=w_scales[:, P * g : P * (g + 1)],
                         rhs=codes[:].bitcast(FP8X4),
                         rhs_scale=scales[:],
                         start=(g == 0),
@@ -162,19 +177,27 @@ def tile_gnn_pb_kernel(
                 in_=result[:].rearrange("m b j s -> m b (j s)"),
             )
 
-        weights = {0: quantise_weight(nc, keep, stage, psum_t, identity, W_bg_p, "bg")}
+        def quantise_weight(raw_tiles, copies, label):
+            return [
+                quantise_weight_tile(
+                    nc, keep, stage, psum_t, identity, raw, copies[j % len(copies)], "%s%d" % (label, j)
+                )
+                for j, raw in enumerate(raw_tiles)
+            ]
+
+        weights = {0: quantise_weight(raw_bg, (nc.scalar.copy,), "bg")}
         affines = {0: affine_bg, 1: affine_decomp, 2: affine_decomp}
         parent_q = {}
-        grouped_next = group_step(steps[0])
+        grouped_next = group_step(0)
         for k, (parent, n, i) in enumerate(steps):
-            grouped = grouped_next
-            if k + 1 < len(steps):
-                grouped_next = group_step(steps[k + 1])
+            grouped = group_step(k) if grouped_next is None else grouped_next
+            grouped_next = group_step(k + 1) if k != 1 and k + 1 < len(steps) else None
             if n is None:
                 parent_q[i] = quantise_maps(nc, parent_codes, grouped, "parent")
                 continue
             part_q = quantise_maps(nc, part_codes, grouped, "part")
             update_part(n, i, parent_q[i], part_q, weights[parent], affines[parent])
             if n == 0 and i == GROUPS - 1:
-                weights[1] = quantise_weight(nc, keep, stage, psum_t, identity, W_decomp_half, "decomp")
+                raw_decomp = [load_weight_tile(nc, keep, W_decomp_half, "decomp", j) for j in range(OUT_TILES)]
+                weights[1] = quantise_weight(raw_decomp, (nc.vector.tensor_copy, nc.scalar.copy), "decomp")
                 weights[2] = weights[1]

@@ -57,14 +57,22 @@ def batch_norm_affine(nc, small, psum_t, identity, table, count):
     return scale, shift
 
 
-def load_weight_tile(nc, w_raw, weight, label, j):
-    raw = w_raw.tile([P, SOURCES * CHANNELS], BF16, name="w_raw_%s%d" % (label, j), align_bytes=DMA_ALIGN)
-    nc.sync.dma_start(out=raw[:], in_=weight.rearrange("(m j) c -> j m c", j=OUT_TILES)[j])
-    return raw
+def load_weight(nc, pool, weight, label, loads):
+    rows = weight.rearrange("(m j) c -> m j c", j=OUT_TILES)
+    share = OUT_TILES // loads
+    tiles = []
+    for i in range(loads):
+        operands = slice(share * i, share * (i + 1))
+        raw = pool.tile(
+            [P, share, SOURCES * CHANNELS], BF16, name="w_raw_%s%d" % (label, i), align_bytes=DMA_ALIGN
+        )
+        nc.sync.dma_start(out=raw[:], in_=rows[:, operands, :])
+        tiles.extend([raw[:, j, :] for j in range(share)])
+    return tiles
 
 
 def quantise_weight_tile(nc, keep, stage, psum_t, identity, raw, copy, label):
-    words = raw[:].bitcast(F32).rearrange("m (g p u) -> m g u p", g=SOURCES, u=2)
+    words = raw.bitcast(F32).rearrange("m (g p u) -> m g u p", g=SOURCES, u=2)
     bank = psum_t.tile([P, SOURCES, 2, P], F32, name="w_bank", tag="turned")
     for g in range(SOURCES):
         for u in range(2):
@@ -80,15 +88,15 @@ def quantise_weight_tile(nc, keep, stage, psum_t, identity, raw, copy, label):
     return codes, scales
 
 
-def load_maps(nc, raw_pool, maps):
-    raw = raw_pool.tile([P, GROUP, PACK, PIXELS], BF16, name="raw", align_bytes=DMA_ALIGN)
+def load_maps(nc, raw_pool, maps, label):
+    raw = raw_pool.tile([P, maps.shape[0], PACK, PIXELS], BF16, name="raw_" + label, align_bytes=DMA_ALIGN)
     nc.sync.dma_start(out=raw[:], in_=maps.rearrange("b (p t) h w -> p b t (h w)", t=PACK))
     return raw
 
 
-def group_maps(nc, stage, raw):
+def group_maps(stage, raw, copy):
     grouped = stage.tile([P, GROUP, PIXELS, PACK], BF16, name="grouped", align_bytes=64)
-    nc.vector.tensor_copy(out=grouped[:], in_=raw[:].rearrange("p b t s -> p b s t"))
+    copy(out=grouped[:], in_=raw.rearrange("p b t s -> p b s t"))
     return grouped
 
 
@@ -110,30 +118,40 @@ def tile_gnn_pb_kernel(
     with ExitStack() as ctx:
         small = ctx.enter_context(tc.tile_pool(name="small", bufs=1))
         keep = ctx.enter_context(tc.tile_pool(name="keep", bufs=1))
-        raw_pool = ctx.enter_context(tc.tile_pool(name="raw_pool", bufs=12))
+        raw_pool = ctx.enter_context(tc.tile_pool(name="raw_pool", bufs=1))
         stage = ctx.enter_context(tc.tile_pool(name="stage", bufs=3))
         parent_codes = ctx.enter_context(tc.tile_pool(name="parent_codes", bufs=2 * GROUPS))
         part_codes = ctx.enter_context(tc.tile_pool(name="part_codes", bufs=4))
-        results = ctx.enter_context(tc.tile_pool(name="results", bufs=10))
+        results = ctx.enter_context(tc.tile_pool(name="results", bufs=9))
         psum_t = ctx.enter_context(tc.psum_pool(name="psum_t", bufs=2))
         psum_acc = ctx.enter_context(tc.psum_pool(name="psum_acc", bufs=6))
 
-        steps = [(0, n, i) for i in range(GROUPS) for n in (None, 0)]
-        for parent, parts in ((1, (1, 2, 3, 4)), (2, (5, 6))):
-            steps.extend([(parent, n, i) for n in (None, *parts) for i in range(GROUPS)])
+        steps = []
+        for parent, parts in ((0, (0,)), (1, (1, 2, 3, 4)), (2, (5, 6))):
+            steps.extend([(parent, n, i) for i in range(GROUPS) for n in (None, parts[0])])
+            steps.extend([(parent, n, i) for n in parts[1:] for i in range(GROUPS)])
 
-        def load_step(k):
-            parent, n, i = steps[k]
-            node = h_nodes[parent] if n is None else p_nodes[n]
-            return load_maps(nc, raw_pool, node[GROUP * i : GROUP * (i + 1)])
+        nodes = {"h": h_nodes.rearrange("n b c h w -> (n b) c h w"), "p": p_nodes.rearrange("n b c h w -> (n b) c h w")}
+        raw_of = {}
 
-        raw_bg, early = [], []
-        for j in range(OUT_TILES):
-            raw_bg.append(load_weight_tile(nc, keep, W_bg_p, "bg", j))
-            if j == 0:
-                bn_table = load_batch_norms(nc, small, (bn_bg_p, bn_decomp_half))
-            if j % 2 == 1:
-                early.append(load_step(len(early)))
+        def load(kind, first, count):
+            raw = load_maps(nc, raw_pool, nodes[kind][first : first + count], "%s%d" % (kind, first))
+            for b in range(0, count, GROUP):
+                raw_of[kind, first + b] = raw[:, b : b + GROUP]
+
+        raw_bg = load_weight(nc, keep, W_bg_p, "bg", 2)
+        bn_table = load_batch_norms(nc, small, (bn_bg_p, bn_decomp_half))
+        for i in range(GROUPS):
+            load("h", GROUP * i, GROUP)
+            load("p", GROUP * i, GROUP)
+        raw_decomp = load_weight(nc, keep, W_decomp_half, "decomp", 1)
+        for i in range(GROUPS):
+            load("h", IMAGES + GROUP * i, GROUP)
+            load("p", IMAGES + GROUP * i, GROUP)
+        load("p", 2 * IMAGES, IMAGES)
+        load("p", 3 * IMAGES, 2 * IMAGES)
+        load("h", 2 * IMAGES, IMAGES)
+        load("p", 5 * IMAGES, 2 * IMAGES)
 
         warm = small.tile([P, 1], F32, name="warm")
         nc.gpsimd.memset(warm[:], 1.0)
@@ -145,7 +163,9 @@ def tile_gnn_pb_kernel(
         affine_decomp = (bn_scale[:, 1, :], bn_shift[:, 1, :])
 
         def group_step(k):
-            return group_maps(nc, stage, early[k] if k < len(early) else load_step(k))
+            parent, n, i = steps[k]
+            raw = raw_of["h", IMAGES * parent + GROUP * i] if n is None else raw_of["p", IMAGES * n + GROUP * i]
+            return group_maps(stage, raw, nc.vector.tensor_copy)
 
         def update_part(n, i, parent_q, part_q, weight, affine):
             scale, shift = affine
@@ -198,6 +218,5 @@ def tile_gnn_pb_kernel(
             part_q = quantise_maps(nc, part_codes, grouped, "part")
             update_part(n, i, parent_q[i], part_q, weights[parent], affines[parent])
             if n == 0 and i == GROUPS - 1:
-                raw_decomp = [load_weight_tile(nc, keep, W_decomp_half, "decomp", j) for j in range(OUT_TILES)]
                 weights[1] = quantise_weight(raw_decomp, (nc.vector.tensor_copy, nc.scalar.copy), "decomp")
                 weights[2] = weights[1]

@@ -191,8 +191,7 @@ def tile_gnn_pb_kernel(
                     bias=shift[:, j : j + 1],
                     scale=scale[:, j : j + 1],
                 )
-            queue = nc.sync if (n >= 2 and i == 1) else nc.scalar
-            queue.dma_start(
+            nc.sync.dma_start(
                 out=out[n, images].rearrange("b (m j) h w -> m b (j h w)", j=OUT_TILES),
                 in_=result[:].rearrange("m b j s -> m b (j s)"),
             )

@@ -122,7 +122,7 @@ def tile_gnn_pb_kernel(
         stage = ctx.enter_context(tc.tile_pool(name="stage", bufs=3))
         parent_codes = ctx.enter_context(tc.tile_pool(name="parent_codes", bufs=2 * GROUPS))
         part_codes = ctx.enter_context(tc.tile_pool(name="part_codes", bufs=4))
-        results = ctx.enter_context(tc.tile_pool(name="results", bufs=9))
+        results = ctx.enter_context(tc.tile_pool(name="results", bufs=5))
         psum_t = ctx.enter_context(tc.psum_pool(name="psum_t", bufs=2))
         psum_acc = ctx.enter_context(tc.psum_pool(name="psum_acc", bufs=6))
 
@@ -139,19 +139,12 @@ def tile_gnn_pb_kernel(
             for b in range(0, count, GROUP):
                 raw_of[kind, first + b] = raw[:, b : b + GROUP]
 
-        raw_bg = load_weight(nc, keep, W_bg_p, "bg", 2)
+        raw_bg = load_weight(nc, keep, W_bg_p, "bg", 1)
         bn_table = load_batch_norms(nc, small, (bn_bg_p, bn_decomp_half))
-        for i in range(GROUPS):
-            load("h", GROUP * i, GROUP)
-            load("p", GROUP * i, GROUP)
-        raw_decomp = load_weight(nc, keep, W_decomp_half, "decomp", 1)
-        for i in range(GROUPS):
-            load("h", IMAGES + GROUP * i, GROUP)
-            load("p", IMAGES + GROUP * i, GROUP)
-        load("p", 2 * IMAGES, IMAGES)
-        load("p", 3 * IMAGES, 2 * IMAGES)
-        load("h", 2 * IMAGES, IMAGES)
-        load("p", 5 * IMAGES, 2 * IMAGES)
+        for k, (parent, n, i) in enumerate(steps):
+            if k == 4:
+                raw_decomp = load_weight(nc, keep, W_decomp_half, "decomp", 1)
+            load(*(("h", IMAGES * parent + GROUP * i) if n is None else ("p", IMAGES * n + GROUP * i)), GROUP)
 
         warm = small.tile([P, 1], F32, name="warm")
         nc.gpsimd.memset(warm[:], 1.0)
@@ -167,10 +160,9 @@ def tile_gnn_pb_kernel(
             raw = raw_of["h", IMAGES * parent + GROUP * i] if n is None else raw_of["p", IMAGES * n + GROUP * i]
             return group_maps(stage, raw, nc.vector.tensor_copy)
 
-        def update_part(n, i, parent_q, part_q, weight, affine):
+        def update_part(result, n, i, parent_q, part_q, weight, affine):
             scale, shift = affine
             images = slice(GROUP * i, GROUP * (i + 1))
-            result = results.tile([P, GROUP, OUT_TILES, PIXELS], F32, name="result", align_bytes=DMA_ALIGN)
             for j in range(OUT_TILES):
                 w_codes, w_scales = weight[j]
                 acc = psum_acc.tile([P, COLS], F32, name="acc")
@@ -185,14 +177,16 @@ def tile_gnn_pb_kernel(
                         stop=(g == SOURCES - 1),
                     )
                 nc.scalar.activation(
-                    out=result[:, :, j, :],
+                    out=result[:, images, j, :],
                     in_=acc[:].rearrange("m (b s) -> m b s", s=PIXELS),
                     func=ACT.Relu,
                     bias=shift[:, j : j + 1],
                     scale=scale[:, j : j + 1],
                 )
+
+        def store_part(n, result):
             nc.sync.dma_start(
-                out=out[n, images].rearrange("b (m j) h w -> m b (j h w)", j=OUT_TILES),
+                out=out[n].rearrange("b (m j) h w -> m b (j h w)", j=OUT_TILES),
                 in_=result[:].rearrange("m b j s -> m b (j s)"),
             )
 
@@ -207,6 +201,7 @@ def tile_gnn_pb_kernel(
         weights = {0: quantise_weight(raw_bg, (nc.scalar.copy,), "bg")}
         affines = {0: affine_bg, 1: affine_decomp, 2: affine_decomp}
         parent_q = {}
+        result_of = {}
         grouped_next = group_step(0)
         for k, (parent, n, i) in enumerate(steps):
             grouped = group_step(k) if grouped_next is None else grouped_next
@@ -215,7 +210,13 @@ def tile_gnn_pb_kernel(
                 parent_q[i] = quantise_maps(nc, parent_codes, grouped, "parent")
                 continue
             part_q = quantise_maps(nc, part_codes, grouped, "part")
-            update_part(n, i, parent_q[i], part_q, weights[parent], affines[parent])
+            if i == 0:
+                result_of[n] = results.tile(
+                    [P, IMAGES, OUT_TILES, PIXELS], F32, name="result", align_bytes=DMA_ALIGN
+                )
+            update_part(result_of[n], n, i, parent_q[i], part_q, weights[parent], affines[parent])
+            if i == GROUPS - 1:
+                store_part(n, result_of[n])
             if n == 0 and i == GROUPS - 1:
                 weights[1] = quantise_weight(raw_decomp, (nc.vector.tensor_copy, nc.scalar.copy), "decomp")
                 weights[2] = weights[1]

from contextlib import ExitStack

import concourse.mybir as mybir
from concourse.masks import make_identity

BF16 = mybir.dt.bfloat16
F32 = mybir.dt.float32
U32 = mybir.dt.uint32
U8 = mybir.dt.uint8
FP8X4 = mybir.dt.float8_e4m3fn_x4
ACT = mybir.ActivationFunctionType

P = 128
PACK = 4
N_PART, N_HALF_BODY, IMAGES, CHANNELS, PIXELS = 7, 3, 8, 512, 128
EPS = 1e-5
BN_ROWS = 4
assert CHANNELS == P * PACK

SOURCES = 2
OUT_TILES = CHANNELS // P
GROUP = 4
GROUPS = IMAGES // GROUP
COLS = GROUP * PIXELS
DMA_ALIGN = 256

FLOPS = 2 * N_PART * IMAGES * PIXELS * CHANNELS * SOURCES * CHANNELS


def load_batch_norms(nc, small, batch_norms):
    table = small.tile([P, CHANNELS], BF16, name="bn_table")
    nc.gpsimd.memset(table[:], 0.0)
    for i, bn in enumerate(batch_norms):
        nc.sync.dma_start(out=table[BN_ROWS * i : BN_ROWS * (i + 1), :], in_=bn)
    return table


def batch_norm_affine(nc, small, psum_t, identity, table, count):
    words = table[:].bitcast(F32).rearrange("r (m u) -> r u m", u=2)
    turned = psum_t.tile([P, 2 * P], F32, name="bn_turned", tag="turned")
    for u in range(2):
        nc.tensor.transpose(turned[:, P * u : P * (u + 1)], words[:, u, :], identity[:])
    rows = small.tile([P, BN_ROWS * count, 2, 2], F32, name="bn_rows")
    pairs = turned[:].bitcast(BF16).rearrange("m (u r e) -> m r u e", u=2, e=2)
    nc.vector.tensor_copy(out=rows[:], in_=pairs[:, 0 : BN_ROWS * count, :, :])
    by_norm = rows[:].rearrange("m (i r) u e -> m r i (u e)", r=BN_ROWS)
    gamma, beta, mean, var = by_norm[:, 0], by_norm[:, 1], by_norm[:, 2], by_norm[:, 3]
    std = small.tile([P, count, OUT_TILES], F32, name="bn_std")
    scale = small.tile([P, count, OUT_TILES], F32, name="bn_scale")
    shift = small.tile([P, count, OUT_TILES], F32, name="bn_shift")
    nc.vector.tensor_scalar_add(out=std[:], in0=var, scalar1=EPS)
    nc.scalar.sqrt(out=std[:], in_=std[:])
    nc.vector.reciprocal(out=scale[:], in_=std[:])
    nc.vector.tensor_mul(out=scale[:], in0=scale[:], in1=gamma)
    nc.vector.tensor_mul(out=shift[:], in0=mean, in1=scale[:])
    nc.vector.tensor_sub(out=shift[:], in0=beta, in1=shift[:])
    return scale, shift


def load_weight(nc, pool, weight, label, loads):
    rows = weight.rearrange("(m j) c -> m j c", j=OUT_TILES)
    share = OUT_TILES // loads
    tiles = []
    for i in range(loads):
        operands = slice(share * i, share * (i + 1))
        raw = pool.tile(
            [P, share, SOURCES * CHANNELS], BF16, name="w_raw_%s%d" % (label, i), align_bytes=DMA_ALIGN
        )
        nc.sync.dma_start(out=raw[:], in_=rows[:, operands, :])
        tiles.extend([raw[:, j, :] for j in range(share)])
    return tiles


def quantise_weight_tile(nc, keep, stage, psum_t, identity, raw, copy, label):
    words = raw.bitcast(F32).rearrange("m (g p u) -> m g u p", g=SOURCES, u=2)
    bank = psum_t.tile([P, SOURCES, 2, P], F32, name="w_bank", tag="turned")
    for g in range(SOURCES):
        for u in range(2):
            nc.tensor.transpose(bank[:, g, u, :], words[:, g, u, :], identity[:])
    grouped = stage.tile([P, SOURCES * P * PACK], BF16, name="w_grouped", align_bytes=64)
    copy(
        out=grouped[:].bitcast(F32).rearrange("p (g m u) -> p g m u", g=SOURCES, u=2),
        in_=bank[:].rearrange("p g u m -> p g m u"),
    )
    codes = keep.tile([P, SOURCES * P], U32, name="w_codes_" + label, align_bytes=64)
    scales = keep.tile([P, SOURCES * P], U8, name="w_scales_" + label, align_bytes=64)
    nc.vector.quantize_mx(out=codes[:].bitcast(FP8X4), scales=scales[:], in_=grouped[:])
    return codes, scales


def load_maps(nc, raw_pool, maps, label):
    raw = raw_pool.tile([P, maps.shape[0], PACK, PIXELS], BF16, name="raw_" + label, align_bytes=DMA_ALIGN)
    nc.sync.dma_start(out=raw[:], in_=maps.rearrange("b (p t) h w -> p b t (h w)", t=PACK))
    return raw


def group_maps(stage, raw, copy):
    grouped = stage.tile([P, GROUP, PIXELS, PACK], BF16, name="grouped", align_bytes=64)
    copy(out=grouped[:], in_=raw.rearrange("p b t s -> p b s t"))
    return grouped


def quantise_maps(nc, code_pool, grouped, label):
    codes = code_pool.tile([P, COLS], U32, name="codes_" + label, align_bytes=64)
    scales = code_pool.tile([P, COLS], U8, name="scales_" + label, align_bytes=64)
    nc.vector.quantize_mx(
        out=codes[:].bitcast(FP8X4),
        scales=scales[:],
        in_=grouped[:].rearrange("p b s t -> p (b s t)"),
    )
    return codes, scales


def tile_gnn_pb_kernel(
    tc, p_nodes, h_nodes, W_decomp_half, bn_decomp_half, W_bg_p, bn_bg_p, out
):
    nc = tc.nc
    with ExitStack() as ctx:
        small = ctx.enter_context(tc.tile_pool(name="small", bufs=1))
        keep = ctx.enter_context(tc.tile_pool(name="keep", bufs=1))
        raw_pool = ctx.enter_context(tc.tile_pool(name="raw_pool", bufs=1))
        stage = ctx.enter_context(tc.tile_pool(name="stage", bufs=3))
        parent_codes = ctx.enter_context(tc.tile_pool(name="parent_codes", bufs=2 * GROUPS))
        part_codes = ctx.enter_context(tc.tile_pool(name="part_codes", bufs=4))
        results = ctx.enter_context(tc.tile_pool(name="results", bufs=5))
        psum_t = ctx.enter_context(tc.psum_pool(name="psum_t", bufs=2))
        psum_acc = ctx.enter_context(tc.psum_pool(name="psum_acc", bufs=6))

        steps = []
        for parent, parts in ((0, (0,)), (1, (1, 2, 3, 4)), (2, (5, 6))):
            steps.extend([(parent, n, i) for i in range(GROUPS) for n in (None, parts[0])])
            steps.extend([(parent, n, i) for n in parts[1:] for i in range(GROUPS)])

        nodes = {"h": h_nodes.rearrange("n b c h w -> (n b) c h w"), "p": p_nodes.rearrange("n b c h w -> (n b) c h w")}
        raw_of = {}

        def load(kind, first, count):
            raw = load_maps(nc, raw_pool, nodes[kind][first : first + count], "%s%d" % (kind, first))
            for b in range(0, count, GROUP):
                raw_of[kind, first + b] = raw[:, b : b + GROUP]

        raw_bg = load_weight(nc, keep, W_bg_p, "bg", 1)
        bn_table = load_batch_norms(nc, small, (bn_bg_p, bn_decomp_half))
        for k, (parent, n, i) in enumerate(steps):
            if k == 4:
                raw_decomp = load_weight(nc, keep, W_decomp_half, "decomp", 1)
            load(*(("h", IMAGES * parent + GROUP * i) if n is None else ("p", IMAGES * n + GROUP * i)), GROUP)

        warm = small.tile([P, 1], F32, name="warm")
        nc.gpsimd.memset(warm[:], 1.0)
        nc.scalar.sqrt(out=warm[:], in_=warm[:])
        identity = small.tile([P, P], F32, name="identity")
        make_identity(nc, identity[:])
        bn_scale, bn_shift = batch_norm_affine(nc, small, psum_t, identity, bn_table, 2)
        affine_bg = (bn_scale[:, 0, :], bn_shift[:, 0, :])
        affine_decomp = (bn_scale[:, 1, :], bn_shift[:, 1, :])

        def group_step(k):
            parent, n, i = steps[k]
            raw = raw_of["h", IMAGES * parent + GROUP * i] if n is None else raw_of["p", IMAGES * n + GROUP * i]
            return group_maps(stage, raw, nc.vector.tensor_copy)

        def update_part(result, n, i, parent_q, part_q, weight, affine):
            scale, shift = affine
            images = slice(GROUP * i, GROUP * (i + 1))
            for j in range(OUT_TILES):
                w_codes, w_scales = weight[j]
                acc = psum_acc.tile([P, COLS], F32, name="acc")
                for g, (codes, scales) in enumerate((parent_q, part_q)):
                    nc.tensor.matmul_mx(
                        out=acc[:],
                        lhsT=w_codes[:, P * g : P * (g + 1)].bitcast(FP8X4),
                        lhsT_scale=w_scales[:, P * g : P * (g + 1)],
                        rhs=codes[:].bitcast(FP8X4),
                        rhs_scale=scales[:],
                        start=(g == 0),
                        stop=(g == SOURCES - 1),
                    )
                nc.scalar.activation(
                    out=result[:, images, j, :],
                    in_=acc[:].rearrange("m (b s) -> m b s", s=PIXELS),
                    func=ACT.Relu,
                    bias=shift[:, j : j + 1],
                    scale=scale[:, j : j + 1],
                )

        def store_part(n, result):
            nc.sync.dma_start(
                out=out[n].rearrange("b (m j) h w -> m b (j h w)", j=OUT_TILES),
                in_=result[:].rearrange("m b j s -> m b (j s)"),
            )

        def quantise_weight(raw_tiles, copies, label):
            return [
                quantise_weight_tile(
                    nc, keep, stage, psum_t, identity, raw, copies[j % len(copies)], "%s%d" % (label, j)
                )
                for j, raw in enumerate(raw_tiles)
            ]

        weights = {0: quantise_weight(raw_bg, (nc.scalar.copy,), "bg")}
        affines = {0: affine_bg, 1: affine_decomp, 2: affine_decomp}
        parent_q = {}
        result_of = {}
        grouped_next = group_step(0)
        for k, (parent, n, i) in enumerate(steps):
            grouped = group_step(k) if grouped_next is None else grouped_next
            grouped_next = group_step(k + 1) if k != 1 and k + 1 < len(steps) else None
            if n is None:
                parent_q[i] = quantise_maps(nc, parent_codes, grouped, "parent")
                continue
            part_q = quantise_maps(nc, part_codes, grouped, "part")
            if i == 0:
                result_of[n] = results.tile(
                    [P, IMAGES, OUT_TILES, PIXELS], F32, name="result", align_bytes=DMA_ALIGN
                )
            update_part(result_of[n], n, i, parent_q[i], part_q, weights[parent], affines[parent])
            if i == GROUPS - 1:
                store_part(n, result_of[n])
            if n == 0 and i == GROUPS - 1:
                weights[1] = quantise_weight(raw_decomp, (nc.vector.tensor_copy, nc.scalar.copy), "decomp")
                weights[2] = weights[1]
